import numpy as np
import ml_dtypes


def mxq(x, axis, fmt="e4m3"):
    dtype, down = {"e4m3": (ml_dtypes.float8_e4m3fn, 7), "e5m2": (ml_dtypes.float8_e5m2, 14)}[fmt]
    v = np.moveaxis(np.asarray(x, np.float32).astype(ml_dtypes.bfloat16).astype(np.float64), axis, -1)
    blocks = v.reshape(v.shape[:-1] + (-1, 32))
    amax = np.abs(blocks).max(-1, keepdims=True)
    byte = np.maximum(np.where(amax > 0, np.frexp(amax)[1] - 1 + 127, 0) - down, 1)
    scale = np.exp2(byte - 127.0)
    codes = (blocks / scale).astype(np.float32).astype(dtype).astype(np.float64)
    return np.moveaxis((codes * scale).reshape(v.shape), -1, axis)


WIDE = False


def mx_kscale(k):
    if not WIDE:
        return np.ones(k)
    levels = np.array([10, -10, 5, -5, 0])
    a = np.random.permutation(np.resize(levels, k // 512 * 4)).reshape(k // 512, 4)
    idx = np.arange(k)
    return np.exp2(a[idx // 512, idx % 128 // 32])


BF16 = ml_dtypes.bfloat16


def bf(x):
    return np.asarray(x, np.float32).astype(BF16)


def f64(x):
    return np.asarray(x).astype(np.float64)


B, C_IN, C_OUT, K, H, W = 2, 1024, 384, 3, 8, 8


def _shift2d(x, dh, dw):
    hh, ww = x.shape[2], x.shape[3]
    ph, pw = abs(dh), abs(dw)
    xp = np.pad(x, ((0, 0), (0, 0), (ph, ph), (pw, pw)))
    return xp[:, :, ph + dh: ph + dh + hh, pw + dw: pw + dw + ww]


def setup_inputs():
    s = mx_kscale(C_IN)
    bound = np.sqrt(2.0) * np.sqrt(3.0 / (C_IN * K))
    return {"x": bf(np.random.standard_normal((B, C_IN, H, W)) * s[None, :, None, None]),
            "weight": bf(np.random.uniform(-bound, bound, (C_OUT, C_IN, K)) / s[None, :, None]),
            "dilation": 1, "step": 1}


def reference(x, weight, dilation, step):
    nb, nc_in, nh, nw = x.shape
    no, nk = weight.shape[0], weight.shape[2]
    c0 = nk // 2
    xq = mxq(f64(x).reshape(nb, nc_in, nh * nw), 1, "e4m3")
    out = np.zeros((nb, no, nh, nw))
    for k in range(nk):
        off = k - c0
        y = mxq(f64(weight)[:, :, k], 1, "e4m3") @ xq
        out = out + _shift2d(y.reshape(nb, no, nh, nw), off * step, off * dilation)
    return out

@@ -1,0 +1,147 @@
+from contextlib import ExitStack
+
+import concourse.mybir as mybir
+from concourse.masks import make_identity
+
+BF16 = mybir.dt.bfloat16
+F32 = mybir.dt.float32
+I32 = mybir.dt.int32
+U32 = mybir.dt.uint32
+U8 = mybir.dt.uint8
+FP8X4 = mybir.dt.float8_e4m3fn_x4
+
+P = 128
+PACK = 4
+PAIRS = PACK // 2
+K_PASS = P * PACK
+
+B, C_IN, C_OUT, TAPS, H, W = 2, 1024, 384, 3, 8, 8
+PIXELS = B * H * W
+PASSES = C_IN // K_PASS
+O_TILES = C_OUT // P
+UNITS = O_TILES * TAPS
+SCALAR_TAP = TAPS - 1
+
+FLOPS = 2 * PIXELS * C_OUT * C_IN * TAPS
+
+
+def tile_skeletonconv_s_kernel(tc, x, weight, dilation, step, out):
+    nc = tc.nc
+    with ExitStack() as ctx:
+        keep = ctx.enter_context(tc.tile_pool(name="keep", bufs=1))
+        raw_pool = ctx.enter_context(tc.tile_pool(name="raw", bufs=O_TILES))
+        sorted_pool = ctx.enter_context(tc.tile_pool(name="sorted", bufs=4))
+        grouped_pool = ctx.enter_context(tc.tile_pool(name="grouped", bufs=3))
+        result_pool = ctx.enter_context(tc.tile_pool(name="result", bufs=2))
+        flipped_pool = ctx.enter_context(tc.psum_pool(name="flipped", bufs=4))
+        acc_pool = ctx.enter_context(tc.psum_pool(name="acc", bufs=2))
+        ctx.enter_context(tc.manual_schedule())
+
+        x_raw = keep.tile([P, B, PASSES, PACK, H * W], BF16)
+        nc.sync.dma_start(
+            out=x_raw[:].rearrange("p b g v s -> p b g (v s)"),
+            in_=x.rearrange("b (g p v) h w -> p b g (v h w)", g=PASSES, p=P, v=PACK),
+        )
+        w_raw = []
+        for ot in range(O_TILES):
+            rows = raw_pool.tile([P, C_IN * TAPS], BF16, name="rows")
+            nc.sync.dma_start(out=rows[:], in_=weight[ot * P : (ot + 1) * P].rearrange("o c t -> o (c t)"))
+            w_raw.append(rows)
+
+        identity = keep.tile([P, P], F32)
+        make_identity(nc, identity[:])
+
+        x_taps = keep.tile([P, TAPS, PASSES, B, H, W, PACK], BF16, align_bytes=64)
+        x_codes = keep.tile([P, TAPS, PASSES * PIXELS], U32, align_bytes=64)
+        x_scales = keep.tile([P, TAPS, PASSES * PIXELS], U8, align_bytes=64)
+        nc.vector.memset(x_taps[:].rearrange("p t g b h w v -> p (t g b h w v)").bitcast(I32), 0)
+        centre = TAPS // 2
+        for g in range(PASSES):
+            nc.vector.tensor_copy(
+                out=x_taps[:, centre, g].rearrange("p b h w v -> p b (h w) v"),
+                in_=x_raw[:, :, g].rearrange("p b v s -> p b s v"),
+            )
+        for t in range(TAPS):
+            if t == centre:
+                continue
+            dh, dw = (t - centre) * step, (t - centre) * dilation
+            h_lo, h_hi = max(0, -dh), H - max(0, dh)
+            w_lo, w_hi = max(0, -dw), W - max(0, dw)
+            shift_engine = nc.scalar.copy if t == SCALAR_TAP else nc.vector.tensor_copy
+            shift_engine(
+                out=x_taps[:, t, :, :, h_lo:h_hi, w_lo:w_hi, :],
+                in_=x_taps[:, centre, :, :, h_lo + dh : h_hi + dh, w_lo + dw : w_hi + dw, :],
+            )
+        for t in range(TAPS):
+            nc.vector.quantize_mx(
+                out=x_codes[:, t, :].bitcast(FP8X4),
+                scales=x_scales[:, t, :],
+                in_=x_taps[:, t].rearrange("p g b h w v -> p (g b h w v)"),
+            )
+
+        w_codes = keep.tile([P, UNITS, PASSES * P], U32, align_bytes=64)
+        w_scales = keep.tile([P, UNITS, PASSES * P], U8, align_bytes=64)
+        w_sorted, w_flipped, w_grouped, acc = {}, {}, {}, {}
+
+        def sort_tap(unit):
+            ot, t = divmod(unit, TAPS)
+            one_tap = sorted_pool.tile([P, PAIRS, C_IN // PAIRS], BF16, name="one_tap")
+            copy = nc.scalar.copy if t == SCALAR_TAP else nc.vector.tensor_copy
+            copy(
+                out=one_tap[:].rearrange("o a (q e) -> o a q e", e=2),
+                in_=w_raw[ot][:].rearrange("o (q a e t) -> o t a q e", a=PAIRS, e=2, t=TAPS)[:, t],
+            )
+            w_sorted[unit] = one_tap
+
+        def flip(unit):
+            words = w_sorted[unit][:].bitcast(F32)
+            flipped = flipped_pool.tile([P, PASSES, PAIRS, P], F32, name="flipped")
+            for g in range(PASSES):
+                for a in range(PAIRS):
+                    nc.tensor.transpose(flipped[:, g, a, :], words[:, a, g * P : (g + 1) * P], identity[:])
+            w_flipped[unit] = flipped
+
+        def group(unit):
+            grouped = grouped_pool.tile([P, PASSES * P * PACK], BF16, name="grouped", align_bytes=64)
+            nc.scalar.copy(
+                out=grouped[:].bitcast(F32).rearrange("p (g o a) -> p g o a", g=PASSES, a=PAIRS),
+                in_=w_flipped[unit][:].rearrange("p g a o -> p g o a"),
+            )
+            w_grouped[unit] = grouped
+
+        def quantise(unit):
+            nc.vector.quantize_mx(
+                out=w_codes[:, unit, :].bitcast(FP8X4), scales=w_scales[:, unit, :], in_=w_grouped[unit][:]
+            )
+
+        def multiply(unit):
+            ot, t = divmod(unit, TAPS)
+            if t == 0:
+                acc[ot] = acc_pool.tile([P, PIXELS], F32, name="acc")
+            for g in range(PASSES):
+                nc.tensor.matmul_mx(
+                    out=acc[ot][:],
+                    lhsT=w_codes[:, unit, g * P : (g + 1) * P].bitcast(FP8X4),
+                    lhsT_scale=w_scales[:, unit, g * P : (g + 1) * P],
+                    rhs=x_codes[:, t, g * PIXELS : (g + 1) * PIXELS].bitcast(FP8X4),
+                    rhs_scale=x_scales[:, t, g * PIXELS : (g + 1) * PIXELS],
+                    start=(t == 0 and g == 0),
+                    stop=(t == TAPS - 1 and g == PASSES - 1),
+                )
+            if t == TAPS - 1:
+                result = result_pool.tile([P, B, H * W], F32, name="result")
+                nc.vector.tensor_copy(out=result[:].rearrange("p b s -> p (b s)"), in_=acc[ot][:])
+                nc.sync.dma_start(
+                    out=out[:, ot * P : (ot + 1) * P].rearrange("b o h w -> o b (h w)"), in_=result[:]
+                )
+
+        for rnd in range(UNITS + 3):
+            if rnd < UNITS:
+                sort_tap(rnd)
+            if 0 <= rnd - 1 < UNITS:
+                flip(rnd - 1)
+            if 0 <= rnd - 2 < UNITS:
+                group(rnd - 2)
+            if 0 <= rnd - 3 < UNITS:
+                quantise(rnd - 3)
+                multiply(rnd - 3)

@@ -12,15 +12,14 @@ FP8X4 = mybir.dt.float8_e4m3fn_x4
 
 P = 128
 PACK = 4
-PAIRS = PACK // 2
 K_PASS = P * PACK
 
 B, C_IN, C_OUT, TAPS, H, W = 2, 1024, 384, 3, 8, 8
 PIXELS = B * H * W
 PASSES = C_IN // K_PASS
 O_TILES = C_OUT // P
-UNITS = O_TILES * TAPS
-SCALAR_TAP = TAPS - 1
+CHUNKS = O_TILES * PASSES
+VECTOR_TAP = 0
 
 FLOPS = 2 * PIXELS * C_OUT * C_IN * TAPS
 
@@ -29,37 +28,40 @@ def tile_skeletonconv_s_kernel(tc, x, weight, dilation, step, out):
     nc = tc.nc
     with ExitStack() as ctx:
         keep = ctx.enter_context(tc.tile_pool(name="keep", bufs=1))
-        raw_pool = ctx.enter_context(tc.tile_pool(name="raw", bufs=O_TILES))
-        sorted_pool = ctx.enter_context(tc.tile_pool(name="sorted", bufs=4))
-        grouped_pool = ctx.enter_context(tc.tile_pool(name="grouped", bufs=3))
+        raw_pool = ctx.enter_context(tc.tile_pool(name="raw", bufs=CHUNKS))
+        grouped_pool = ctx.enter_context(tc.tile_pool(name="grouped", bufs=3 * TAPS))
         result_pool = ctx.enter_context(tc.tile_pool(name="result", bufs=2))
-        flipped_pool = ctx.enter_context(tc.psum_pool(name="flipped", bufs=4))
+        flipped_pool = ctx.enter_context(tc.psum_pool(name="flipped", bufs=2 * TAPS))
         acc_pool = ctx.enter_context(tc.psum_pool(name="acc", bufs=2))
         ctx.enter_context(tc.manual_schedule())
 
         x_raw = keep.tile([P, B, PASSES, PACK, H * W], BF16)
         nc.sync.dma_start(
-            out=x_raw[:].rearrange("p b g v s -> p b g (v s)"),
-            in_=x.rearrange("b (g p v) h w -> p b g (v h w)", g=PASSES, p=P, v=PACK),
+            out=x_raw[:].rearrange("p b g u s -> p (b g u) s"),
+            in_=x.rearrange("b (g u p) h w -> p (b g u) (h w)", g=PASSES, u=PACK, p=P),
         )
         w_raw = []
-        for ot in range(O_TILES):
-            rows = raw_pool.tile([P, C_IN * TAPS], BF16, name="rows")
-            nc.sync.dma_start(out=rows[:], in_=weight[ot * P : (ot + 1) * P].rearrange("o c t -> o (c t)"))
+        for chunk in range(CHUNKS):
+            ot, g = divmod(chunk, PASSES)
+            rows = raw_pool.tile([P, K_PASS * TAPS], BF16, name="rows")
+            nc.sync.dma_start(
+                out=rows[:],
+                in_=weight[ot * P : (ot + 1) * P, g * K_PASS : (g + 1) * K_PASS].rearrange("o c t -> o (c t)"),
+            )
             w_raw.append(rows)
 
-        identity = keep.tile([P, P], F32)
+        identity = keep.tile([P, P], BF16)
         make_identity(nc, identity[:])
 
         x_taps = keep.tile([P, TAPS, PASSES, B, H, W, PACK], BF16, align_bytes=64)
-        x_codes = keep.tile([P, TAPS, PASSES * PIXELS], U32, align_bytes=64)
-        x_scales = keep.tile([P, TAPS, PASSES * PIXELS], U8, align_bytes=64)
-        nc.vector.memset(x_taps[:].rearrange("p t g b h w v -> p (t g b h w v)").bitcast(I32), 0)
+        x_codes = keep.tile([P, TAPS, PASSES, PIXELS], U32, align_bytes=64)
+        x_scales = keep.tile([P, TAPS, PASSES, PIXELS], U8, align_bytes=64)
+        nc.vector.memset(x_taps[:].rearrange("p t g b h w u -> p (t g b h w u)").bitcast(I32), 0)
         centre = TAPS // 2
         for g in range(PASSES):
             nc.vector.tensor_copy(
-                out=x_taps[:, centre, g].rearrange("p b h w v -> p b (h w) v"),
-                in_=x_raw[:, :, g].rearrange("p b v s -> p b s v"),
+                out=x_taps[:, centre, g].rearrange("p b h w u -> p b (h w) u"),
+                in_=x_raw[:, :, g].rearrange("p b u s -> p b s u"),
             )
         for t in range(TAPS):
             if t == centre:
@@ -67,81 +69,71 @@ def tile_skeletonconv_s_kernel(tc, x, weight, dilation, step, out):
             dh, dw = (t - centre) * step, (t - centre) * dilation
             h_lo, h_hi = max(0, -dh), H - max(0, dh)
             w_lo, w_hi = max(0, -dw), W - max(0, dw)
-            shift_engine = nc.scalar.copy if t == SCALAR_TAP else nc.vector.tensor_copy
-            shift_engine(
+            shift = nc.vector.tensor_copy if t == VECTOR_TAP else nc.scalar.copy
+            shift(
                 out=x_taps[:, t, :, :, h_lo:h_hi, w_lo:w_hi, :],
                 in_=x_taps[:, centre, :, :, h_lo + dh : h_hi + dh, w_lo + dw : w_hi + dw, :],
             )
         for t in range(TAPS):
             nc.vector.quantize_mx(
-                out=x_codes[:, t, :].bitcast(FP8X4),
-                scales=x_scales[:, t, :],
-                in_=x_taps[:, t].rearrange("p g b h w v -> p (g b h w v)"),
+                out=x_codes[:, t].rearrange("p g n -> p (g n)").bitcast(FP8X4),
+                scales=x_scales[:, t].rearrange("p g n -> p (g n)"),
+                in_=x_taps[:, t].rearrange("p g b h w u -> p (g b h w u)"),
             )
 
-        w_codes = keep.tile([P, UNITS, PASSES * P], U32, align_bytes=64)
-        w_scales = keep.tile([P, UNITS, PASSES * P], U8, align_bytes=64)
-        w_sorted, w_flipped, w_grouped, acc = {}, {}, {}, {}
+        w_codes = keep.tile([P, CHUNKS, TAPS, P], U32, align_bytes=64)
+        w_scales = keep.tile([P, CHUNKS, TAPS, P], U8, align_bytes=64)
+        w_flipped, w_grouped, acc = {}, {}, {}
 
-        def sort_tap(unit):
-            ot, t = divmod(unit, TAPS)
-            one_tap = sorted_pool.tile([P, PAIRS, C_IN // PAIRS], BF16, name="one_tap")
-            copy = nc.scalar.copy if t == SCALAR_TAP else nc.vector.tensor_copy
-            copy(
-                out=one_tap[:].rearrange("o a (q e) -> o a q e", e=2),
-                in_=w_raw[ot][:].rearrange("o (q a e t) -> o t a q e", a=PAIRS, e=2, t=TAPS)[:, t],
-            )
-            w_sorted[unit] = one_tap
+        def flip(chunk):
+            by_tap = w_raw[chunk][:].rearrange("o (u c t) -> o t u c", u=PACK, t=TAPS)
+            for t in range(TAPS):
+                flipped = flipped_pool.tile([P, PACK, P], BF16, name="flipped")
+                for u in range(PACK):
+                    nc.tensor.transpose(flipped[:, u, :], by_tap[:, t, u], identity[:])
+                w_flipped[chunk, t] = flipped
 
-        def flip(unit):
-            words = w_sorted[unit][:].bitcast(F32)
-            flipped = flipped_pool.tile([P, PASSES, PAIRS, P], F32, name="flipped")
-            for g in range(PASSES):
-                for a in range(PAIRS):
-                    nc.tensor.transpose(flipped[:, g, a, :], words[:, a, g * P : (g + 1) * P], identity[:])
-            w_flipped[unit] = flipped
+        def group(chunk):
+            for t in range(TAPS):
+                grouped = grouped_pool.tile([P, P, PACK], BF16, name="grouped", align_bytes=64)
+                copy = nc.vector.tensor_copy if t == VECTOR_TAP else nc.scalar.copy
+                copy(out=grouped[:], in_=w_flipped[chunk, t][:].rearrange("p u o -> p o u"))
+                w_grouped[chunk, t] = grouped
 
-        def group(unit):
-            grouped = grouped_pool.tile([P, PASSES * P * PACK], BF16, name="grouped", align_bytes=64)
-            nc.scalar.copy(
-                out=grouped[:].bitcast(F32).rearrange("p (g o a) -> p g o a", g=PASSES, a=PAIRS),
-                in_=w_flipped[unit][:].rearrange("p g a o -> p g o a"),
-            )
-            w_grouped[unit] = grouped
+        def quantise(chunk):
+            for t in range(TAPS):
+                nc.vector.quantize_mx(
+                    out=w_codes[:, chunk, t].bitcast(FP8X4),
+                    scales=w_scales[:, chunk, t],
+                    in_=w_grouped[chunk, t][:].rearrange("p o u -> p (o u)"),
+                )
 
-        def quantise(unit):
-            nc.vector.quantize_mx(
-                out=w_codes[:, unit, :].bitcast(FP8X4), scales=w_scales[:, unit, :], in_=w_grouped[unit][:]
-            )
-
-        def multiply(unit):
-            ot, t = divmod(unit, TAPS)
-            if t == 0:
+        def multiply(chunk):
+            ot, g = divmod(chunk, PASSES)
+            if g == 0:
                 acc[ot] = acc_pool.tile([P, PIXELS], F32, name="acc")
-            for g in range(PASSES):
+            for t in range(TAPS):
                 nc.tensor.matmul_mx(
                     out=acc[ot][:],
-                    lhsT=w_codes[:, unit, g * P : (g + 1) * P].bitcast(FP8X4),
-                    lhsT_scale=w_scales[:, unit, g * P : (g + 1) * P],
-                    rhs=x_codes[:, t, g * PIXELS : (g + 1) * PIXELS].bitcast(FP8X4),
-                    rhs_scale=x_scales[:, t, g * PIXELS : (g + 1) * PIXELS],
-                    start=(t == 0 and g == 0),
-                    stop=(t == TAPS - 1 and g == PASSES - 1),
+                    lhsT=w_codes[:, chunk, t].bitcast(FP8X4),
+                    lhsT_scale=w_scales[:, chunk, t],
+                    rhs=x_codes[:, t, g].bitcast(FP8X4),
+                    rhs_scale=x_scales[:, t, g],
+                    start=(g == 0 and t == 0),
+                    stop=(g == PASSES - 1 and t == TAPS - 1),
                 )
-            if t == TAPS - 1:
+            if g == PASSES - 1:
                 result = result_pool.tile([P, B, H * W], F32, name="result")
                 nc.vector.tensor_copy(out=result[:].rearrange("p b s -> p (b s)"), in_=acc[ot][:])
                 nc.sync.dma_start(
                     out=out[:, ot * P : (ot + 1) * P].rearrange("b o h w -> o b (h w)"), in_=result[:]
                 )
 
-        for rnd in range(UNITS + 3):
-            if rnd < UNITS:
-                sort_tap(rnd)
-            if 0 <= rnd - 1 < UNITS:
-                flip(rnd - 1)
-            if 0 <= rnd - 2 < UNITS:
-                group(rnd - 2)
-            if 0 <= rnd - 3 < UNITS:
-                quantise(rnd - 3)
-                multiply(rnd - 3)
+        for rnd in range(CHUNKS + 2):
+            if rnd < CHUNKS:
+                flip(rnd)
+            if 0 <= rnd - 1 < CHUNKS:
+                group(rnd - 1)
+            if 0 <= rnd - 2 < CHUNKS:
+                quantise(rnd - 2)
+                multiply(rnd - 2)

@@ -19,7 +19,9 @@ PIXELS = B * H * W
 PASSES = C_IN // K_PASS
 O_TILES = C_OUT // P
 CHUNKS = O_TILES * PASSES
-VECTOR_TAP = 0
+VECTOR_TAP = 1
+X_ROUND = 4
+PSUM_BANKS = 8
 
 FLOPS = 2 * PIXELS * C_OUT * C_IN * TAPS
 
@@ -30,18 +32,19 @@ def tile_skeletonconv_s_kernel(tc, x, weight, dilation, step, out):
         keep = ctx.enter_context(tc.tile_pool(name="keep", bufs=1))
         raw_pool = ctx.enter_context(tc.tile_pool(name="raw", bufs=CHUNKS))
         grouped_pool = ctx.enter_context(tc.tile_pool(name="grouped", bufs=3 * TAPS))
-        result_pool = ctx.enter_context(tc.tile_pool(name="result", bufs=2))
-        flipped_pool = ctx.enter_context(tc.psum_pool(name="flipped", bufs=2 * TAPS))
-        acc_pool = ctx.enter_context(tc.psum_pool(name="acc", bufs=2))
+        result_pool = ctx.enter_context(tc.tile_pool(name="result", bufs=O_TILES))
+        flipped_pool = ctx.enter_context(tc.psum_pool(name="flipped", bufs=PSUM_BANKS - O_TILES))
+        acc_pool = ctx.enter_context(tc.psum_pool(name="acc", bufs=O_TILES))
         ctx.enter_context(tc.manual_schedule())
 
         x_raw = keep.tile([P, B, PASSES, PACK, H * W], BF16)
-        nc.sync.dma_start(
-            out=x_raw[:].rearrange("p b g u s -> p (b g u) s"),
-            in_=x.rearrange("b (g u p) h w -> p (b g u) (h w)", g=PASSES, u=PACK, p=P),
-        )
         w_raw = []
         for chunk in range(CHUNKS):
+            if chunk == X_ROUND:
+                nc.sync.dma_start(
+                    out=x_raw[:].rearrange("p b g u s -> p (b g u) s"),
+                    in_=x.rearrange("b (g u p) h w -> p (b g u) (h w)", g=PASSES, u=PACK, p=P),
+                )
             ot, g = divmod(chunk, PASSES)
             rows = raw_pool.tile([P, K_PASS * TAPS], BF16, name="rows")
             nc.sync.dma_start(
@@ -58,28 +61,32 @@ def tile_skeletonconv_s_kernel(tc, x, weight, dilation, step, out):
         x_scales = keep.tile([P, TAPS, PASSES, PIXELS], U8, align_bytes=64)
         nc.vector.memset(x_taps[:].rearrange("p t g b h w u -> p (t g b h w u)").bitcast(I32), 0)
         centre = TAPS // 2
-        for g in range(PASSES):
-            nc.vector.tensor_copy(
-                out=x_taps[:, centre, g].rearrange("p b h w u -> p b (h w) u"),
-                in_=x_raw[:, :, g].rearrange("p b u s -> p b s u"),
-            )
-        for t in range(TAPS):
-            if t == centre:
-                continue
-            dh, dw = (t - centre) * step, (t - centre) * dilation
-            h_lo, h_hi = max(0, -dh), H - max(0, dh)
-            w_lo, w_hi = max(0, -dw), W - max(0, dw)
-            shift = nc.vector.tensor_copy if t == VECTOR_TAP else nc.scalar.copy
-            shift(
-                out=x_taps[:, t, :, :, h_lo:h_hi, w_lo:w_hi, :],
-                in_=x_taps[:, centre, :, :, h_lo + dh : h_hi + dh, w_lo + dw : w_hi + dw, :],
-            )
-        for t in range(TAPS):
-            nc.vector.quantize_mx(
-                out=x_codes[:, t].rearrange("p g n -> p (g n)").bitcast(FP8X4),
-                scales=x_scales[:, t].rearrange("p g n -> p (g n)"),
-                in_=x_taps[:, t].rearrange("p g b h w u -> p (g b h w u)"),
-            )
+
+        def shift_x():
+            for g in range(PASSES):
+                nc.vector.tensor_copy(
+                    out=x_taps[:, centre, g].rearrange("p b h w u -> p b (h w) u"),
+                    in_=x_raw[:, :, g].rearrange("p b u s -> p b s u"),
+                )
+            for t in range(TAPS):
+                if t == centre:
+                    continue
+                dh, dw = (t - centre) * step, (t - centre) * dilation
+                h_lo, h_hi = max(0, -dh), H - max(0, dh)
+                w_lo, w_hi = max(0, -dw), W - max(0, dw)
+                shift = nc.vector.tensor_copy if t < centre else nc.scalar.copy
+                shift(
+                    out=x_taps[:, t, :, :, h_lo:h_hi, w_lo:w_hi, :],
+                    in_=x_taps[:, centre, :, :, h_lo + dh : h_hi + dh, w_lo + dw : w_hi + dw, :],
+                )
+
+        def quantise_x():
+            for t in range(TAPS):
+                nc.vector.quantize_mx(
+                    out=x_codes[:, t].rearrange("p g n -> p (g n)").bitcast(FP8X4),
+                    scales=x_scales[:, t].rearrange("p g n -> p (g n)"),
+                    in_=x_taps[:, t].rearrange("p g b h w u -> p (g b h w u)"),
+                )
 
         w_codes = keep.tile([P, CHUNKS, TAPS, P], U32, align_bytes=64)
         w_scales = keep.tile([P, CHUNKS, TAPS, P], U8, align_bytes=64)
@@ -124,7 +131,7 @@ def tile_skeletonconv_s_kernel(tc, x, weight, dilation, step, out):
                 )
             if g == PASSES - 1:
                 result = result_pool.tile([P, B, H * W], F32, name="result")
-                nc.vector.tensor_copy(out=result[:].rearrange("p b s -> p (b s)"), in_=acc[ot][:])
+                nc.scalar.copy(out=result[:].rearrange("p b s -> p (b s)"), in_=acc[ot][:])
                 nc.sync.dma_start(
                     out=out[:, ot * P : (ot + 1) * P].rearrange("b o h w -> o b (h w)"), in_=result[:]
                 )
@@ -136,4 +143,9 @@ def tile_skeletonconv_s_kernel(tc, x, weight, dilation, step, out):
                 group(rnd - 1)
             if 0 <= rnd - 2 < CHUNKS:
                 quantise(rnd - 2)
-                multiply(rnd - 2)
+            if rnd == X_ROUND:
+                shift_x()
+            if rnd == X_ROUND + 1:
+                quantise_x()
+        for chunk in range(CHUNKS):
+            multiply(chunk)

@@ -13,6 +13,7 @@ FP8X4 = mybir.dt.float8_e4m3fn_x4
 P = 128
 PACK = 4
 K_PASS = P * PACK
+HALVES = 2
 
 B, C_IN, C_OUT, TAPS, H, W = 2, 1024, 384, 3, 8, 8
 PIXELS = B * H * W
@@ -46,11 +47,15 @@ def tile_skeletonconv_s_kernel(tc, x, weight, dilation, step, out):
                     in_=x.rearrange("b (g u p) h w -> p (b g u) (h w)", g=PASSES, u=PACK, p=P),
                 )
             ot, g = divmod(chunk, PASSES)
-            rows = raw_pool.tile([P, K_PASS * TAPS], BF16, name="rows")
-            nc.sync.dma_start(
-                out=rows[:],
-                in_=weight[ot * P : (ot + 1) * P, g * K_PASS : (g + 1) * K_PASS].rearrange("o c t -> o (c t)"),
-            )
+            rows = raw_pool.tile([P, HALVES, K_PASS // HALVES * TAPS], BF16, name="rows")
+            for z in range(HALVES):
+                first = g * K_PASS + z * (K_PASS // HALVES)
+                nc.sync.dma_start(
+                    out=rows[z:P:HALVES],
+                    in_=weight[ot * P : (ot + 1) * P, first : first + K_PASS // HALVES].rearrange(
+                        "(r j) c t -> j r (c t)", r=HALVES
+                    ),
+                )
             w_raw.append(rows)
 
         identity = keep.tile([P, P], BF16)
@@ -59,14 +64,14 @@ def tile_skeletonconv_s_kernel(tc, x, weight, dilation, step, out):
         x_taps = keep.tile([P, TAPS, PASSES, B, H, W, PACK], BF16, align_bytes=64)
         x_codes = keep.tile([P, TAPS, PASSES, PIXELS], U32, align_bytes=64)
         x_scales = keep.tile([P, TAPS, PASSES, PIXELS], U8, align_bytes=64)
-        nc.vector.memset(x_taps[:].rearrange("p t g b h w u -> p (t g b h w u)").bitcast(I32), 0)
+        nc.vector.memset(x_taps[:].rearrange("p t g b h w v -> p (t g b h w v)").bitcast(I32), 0)
         centre = TAPS // 2
 
         def shift_x():
             for g in range(PASSES):
                 nc.vector.tensor_copy(
-                    out=x_taps[:, centre, g].rearrange("p b h w u -> p b (h w) u"),
-                    in_=x_raw[:, :, g].rearrange("p b u s -> p b s u"),
+                    out=x_taps[:, centre, g].rearrange("p b h w (y z) -> p b (h w) y z", z=HALVES),
+                    in_=x_raw[:, :, g].rearrange("p b (z y) s -> p b s y z", z=HALVES),
                 )
             for t in range(TAPS):
                 if t == centre:
@@ -85,7 +90,7 @@ def tile_skeletonconv_s_kernel(tc, x, weight, dilation, step, out):
                 nc.vector.quantize_mx(
                     out=x_codes[:, t].rearrange("p g n -> p (g n)").bitcast(FP8X4),
                     scales=x_scales[:, t].rearrange("p g n -> p (g n)"),
-                    in_=x_taps[:, t].rearrange("p g b h w u -> p (g b h w u)"),
+                    in_=x_taps[:, t].rearrange("p g b h w v -> p (g b h w v)"),
                 )
 
         w_codes = keep.tile([P, CHUNKS, TAPS, P], U32, align_bytes=64)
@@ -93,18 +98,22 @@ def tile_skeletonconv_s_kernel(tc, x, weight, dilation, step, out):
         w_flipped, w_grouped, acc = {}, {}, {}
 
         def flip(chunk):
-            by_tap = w_raw[chunk][:].rearrange("o (u c t) -> o t u c", u=PACK, t=TAPS)
+            by_tap = w_raw[chunk][:].rearrange("q r (y c t) -> q r t y c", y=HALVES, t=TAPS)
             for t in range(TAPS):
-                flipped = flipped_pool.tile([P, PACK, P], BF16, name="flipped")
-                for u in range(PACK):
-                    nc.tensor.transpose(flipped[:, u, :], by_tap[:, t, u], identity[:])
+                flipped = flipped_pool.tile([P, HALVES, HALVES, P], BF16, name="flipped")
+                for y in range(HALVES):
+                    for r in range(HALVES):
+                        nc.tensor.transpose(flipped[:, y, r, :], by_tap[:, r, t, y], identity[:])
                 w_flipped[chunk, t] = flipped
 
         def group(chunk):
             for t in range(TAPS):
-                grouped = grouped_pool.tile([P, P, PACK], BF16, name="grouped", align_bytes=64)
+                grouped = grouped_pool.tile([P, P * PACK], BF16, name="grouped", align_bytes=64)
                 copy = nc.vector.tensor_copy if t == VECTOR_TAP else nc.scalar.copy
-                copy(out=grouped[:], in_=w_flipped[chunk, t][:].rearrange("p u o -> p o u"))
+                copy(
+                    out=grouped[:].bitcast(F32).rearrange("p (o y) -> p o y", y=HALVES),
+                    in_=w_flipped[chunk, t][:].rearrange("p y r q -> p y (r q)").bitcast(F32).rearrange("p y o -> p o y"),
+                )
                 w_grouped[chunk, t] = grouped
 
         def quantise(chunk):
@@ -112,7 +121,7 @@ def tile_skeletonconv_s_kernel(tc, x, weight, dilation, step, out):
                 nc.vector.quantize_mx(
                     out=w_codes[:, chunk, t].bitcast(FP8X4),
                     scales=w_scales[:, chunk, t],
-                    in_=w_grouped[chunk, t][:].rearrange("p o u -> p (o u)"),
+                    in_=w_grouped[chunk, t][:],
                 )
 
         def multiply(chunk):

@@ -20,7 +20,6 @@ PIXELS = B * H * W
 PASSES = C_IN // K_PASS
 O_TILES = C_OUT // P
 CHUNKS = O_TILES * PASSES
-VECTOR_TAP = 1
 X_ROUND = 4
 PSUM_BANKS = 8
 
@@ -79,8 +78,7 @@ def tile_skeletonconv_s_kernel(tc, x, weight, dilation, step, out):
                 dh, dw = (t - centre) * step, (t - centre) * dilation
                 h_lo, h_hi = max(0, -dh), H - max(0, dh)
                 w_lo, w_hi = max(0, -dw), W - max(0, dw)
-                shift = nc.vector.tensor_copy if t < centre else nc.scalar.copy
-                shift(
+                nc.vector.tensor_copy(
                     out=x_taps[:, t, :, :, h_lo:h_hi, w_lo:w_hi, :],
                     in_=x_taps[:, centre, :, :, h_lo + dh : h_hi + dh, w_lo + dw : w_hi + dw, :],
                 )
@@ -109,8 +107,7 @@ def tile_skeletonconv_s_kernel(tc, x, weight, dilation, step, out):
         def group(chunk):
             for t in range(TAPS):
                 grouped = grouped_pool.tile([P, P * PACK], BF16, name="grouped", align_bytes=64)
-                copy = nc.vector.tensor_copy if t == VECTOR_TAP else nc.scalar.copy
-                copy(
+                nc.scalar.copy(
                     out=grouped[:].bitcast(F32).rearrange("p (o y) -> p o y", y=HALVES),
                     in_=w_flipped[chunk, t][:].rearrange("p y r q -> p y (r q)").bitcast(F32).rearrange("p y o -> p o y"),
                 )

@@ -20,7 +20,7 @@ PIXELS = B * H * W
 PASSES = C_IN // K_PASS
 O_TILES = C_OUT // P
 CHUNKS = O_TILES * PASSES
-X_ROUND = 4
+X_ROUND = 2
 PSUM_BANKS = 8
 
 FLOPS = 2 * PIXELS * C_OUT * C_IN * TAPS

@@ -35,7 +35,6 @@ def tile_skeletonconv_s_kernel(tc, x, weight, dilation, step, out):
         result_pool = ctx.enter_context(tc.tile_pool(name="result", bufs=O_TILES))
         flipped_pool = ctx.enter_context(tc.psum_pool(name="flipped", bufs=PSUM_BANKS - O_TILES))
         acc_pool = ctx.enter_context(tc.psum_pool(name="acc", bufs=O_TILES))
-        ctx.enter_context(tc.manual_schedule())
 
         x_raw = keep.tile([P, B, PASSES, PACK, H * W], BF16)
         w_raw = []

from contextlib import ExitStack

import concourse.mybir as mybir
from concourse.masks import make_identity

BF16 = mybir.dt.bfloat16
F32 = mybir.dt.float32
I32 = mybir.dt.int32
U32 = mybir.dt.uint32
U8 = mybir.dt.uint8
FP8X4 = mybir.dt.float8_e4m3fn_x4

P = 128
PACK = 4
K_PASS = P * PACK
HALVES = 2

B, C_IN, C_OUT, TAPS, H, W = 2, 1024, 384, 3, 8, 8
PIXELS = B * H * W
PASSES = C_IN // K_PASS
O_TILES = C_OUT // P
CHUNKS = O_TILES * PASSES
X_ROUND = 2
PSUM_BANKS = 8

FLOPS = 2 * PIXELS * C_OUT * C_IN * TAPS


def tile_skeletonconv_s_kernel(tc, x, weight, dilation, step, out):
    nc = tc.nc
    with ExitStack() as ctx:
        keep = ctx.enter_context(tc.tile_pool(name="keep", bufs=1))
        raw_pool = ctx.enter_context(tc.tile_pool(name="raw", bufs=CHUNKS))
        grouped_pool = ctx.enter_context(tc.tile_pool(name="grouped", bufs=3 * TAPS))
        result_pool = ctx.enter_context(tc.tile_pool(name="result", bufs=O_TILES))
        flipped_pool = ctx.enter_context(tc.psum_pool(name="flipped", bufs=PSUM_BANKS - O_TILES))
        acc_pool = ctx.enter_context(tc.psum_pool(name="acc", bufs=O_TILES))

        x_raw = keep.tile([P, B, PASSES, PACK, H * W], BF16)
        w_raw = []
        for chunk in range(CHUNKS):
            if chunk == X_ROUND:
                nc.sync.dma_start(
                    out=x_raw[:].rearrange("p b g u s -> p (b g u) s"),
                    in_=x.rearrange("b (g u p) h w -> p (b g u) (h w)", g=PASSES, u=PACK, p=P),
                )
            ot, g = divmod(chunk, PASSES)
            rows = raw_pool.tile([P, HALVES, K_PASS // HALVES * TAPS], BF16, name="rows")
            for z in range(HALVES):
                first = g * K_PASS + z * (K_PASS // HALVES)
                nc.sync.dma_start(
                    out=rows[z:P:HALVES],
                    in_=weight[ot * P : (ot + 1) * P, first : first + K_PASS // HALVES].rearrange(
                        "(r j) c t -> j r (c t)", r=HALVES
                    ),
                )
            w_raw.append(rows)

        identity = keep.tile([P, P], BF16)
        make_identity(nc, identity[:])

        x_taps = keep.tile([P, TAPS, PASSES, B, H, W, PACK], BF16, align_bytes=64)
        x_codes = keep.tile([P, TAPS, PASSES, PIXELS], U32, align_bytes=64)
        x_scales = keep.tile([P, TAPS, PASSES, PIXELS], U8, align_bytes=64)
        nc.vector.memset(x_taps[:].rearrange("p t g b h w v -> p (t g b h w v)").bitcast(I32), 0)
        centre = TAPS // 2

        def shift_x():
            for g in range(PASSES):
                nc.vector.tensor_copy(
                    out=x_taps[:, centre, g].rearrange("p b h w (y z) -> p b (h w) y z", z=HALVES),
                    in_=x_raw[:, :, g].rearrange("p b (z y) s -> p b s y z", z=HALVES),
                )
            for t in range(TAPS):
                if t == centre:
                    continue
                dh, dw = (t - centre) * step, (t - centre) * dilation
                h_lo, h_hi = max(0, -dh), H - max(0, dh)
                w_lo, w_hi = max(0, -dw), W - max(0, dw)
                nc.vector.tensor_copy(
                    out=x_taps[:, t, :, :, h_lo:h_hi, w_lo:w_hi, :],
                    in_=x_taps[:, centre, :, :, h_lo + dh : h_hi + dh, w_lo + dw : w_hi + dw, :],
                )

        def quantise_x():
            for t in range(TAPS):
                nc.vector.quantize_mx(
                    out=x_codes[:, t].rearrange("p g n -> p (g n)").bitcast(FP8X4),
                    scales=x_scales[:, t].rearrange("p g n -> p (g n)"),
                    in_=x_taps[:, t].rearrange("p g b h w v -> p (g b h w v)"),
                )

        w_codes = keep.tile([P, CHUNKS, TAPS, P], U32, align_bytes=64)
        w_scales = keep.tile([P, CHUNKS, TAPS, P], U8, align_bytes=64)
        w_flipped, w_grouped, acc = {}, {}, {}

        def flip(chunk):
            by_tap = w_raw[chunk][:].rearrange("q r (y c t) -> q r t y c", y=HALVES, t=TAPS)
            for t in range(TAPS):
                flipped = flipped_pool.tile([P, HALVES, HALVES, P], BF16, name="flipped")
                for y in range(HALVES):
                    for r in range(HALVES):
                        nc.tensor.transpose(flipped[:, y, r, :], by_tap[:, r, t, y], identity[:])
                w_flipped[chunk, t] = flipped

        def group(chunk):
            for t in range(TAPS):
                grouped = grouped_pool.tile([P, P * PACK], BF16, name="grouped", align_bytes=64)
                nc.scalar.copy(
                    out=grouped[:].bitcast(F32).rearrange("p (o y) -> p o y", y=HALVES),
                    in_=w_flipped[chunk, t][:].rearrange("p y r q -> p y (r q)").bitcast(F32).rearrange("p y o -> p o y"),
                )
                w_grouped[chunk, t] = grouped

        def quantise(chunk):
            for t in range(TAPS):
                nc.vector.quantize_mx(
                    out=w_codes[:, chunk, t].bitcast(FP8X4),
                    scales=w_scales[:, chunk, t],
                    in_=w_grouped[chunk, t][:],
                )

        def multiply(chunk):
            ot, g = divmod(chunk, PASSES)
            if g == 0:
                acc[ot] = acc_pool.tile([P, PIXELS], F32, name="acc")
            for t in range(TAPS):
                nc.tensor.matmul_mx(
                    out=acc[ot][:],
                    lhsT=w_codes[:, chunk, t].bitcast(FP8X4),
                    lhsT_scale=w_scales[:, chunk, t],
                    rhs=x_codes[:, t, g].bitcast(FP8X4),
                    rhs_scale=x_scales[:, t, g],
                    start=(g == 0 and t == 0),
                    stop=(g == PASSES - 1 and t == TAPS - 1),
                )
            if g == PASSES - 1:
                result = result_pool.tile([P, B, H * W], F32, name="result")
                nc.scalar.copy(out=result[:].rearrange("p b s -> p (b s)"), in_=acc[ot][:])
                nc.sync.dma_start(
                    out=out[:, ot * P : (ot + 1) * P].rearrange("b o h w -> o b (h w)"), in_=result[:]
                )

        for rnd in range(CHUNKS + 2):
            if rnd < CHUNKS:
                flip(rnd)
            if 0 <= rnd - 1 < CHUNKS:
                group(rnd - 1)
            if 0 <= rnd - 2 < CHUNKS:
                quantise(rnd - 2)
            if rnd == X_ROUND:
                shift_x()
            if rnd == X_ROUND + 1:
                quantise_x()
        for chunk in range(CHUNKS):
            multiply(chunk)
